import numpy as np
import ml_dtypes


def mxq(x, axis, fmt="e4m3"):
    dtype, down = {"e4m3": (ml_dtypes.float8_e4m3fn, 7), "e5m2": (ml_dtypes.float8_e5m2, 14)}[fmt]
    v = np.moveaxis(np.asarray(x, np.float32).astype(ml_dtypes.bfloat16).astype(np.float64), axis, -1)
    blocks = v.reshape(v.shape[:-1] + (-1, 32))
    amax = np.abs(blocks).max(-1, keepdims=True)
    byte = np.maximum(np.where(amax > 0, np.frexp(amax)[1] - 1 + 127, 0) - down, 1)
    scale = np.exp2(byte - 127.0)
    codes = (blocks / scale).astype(np.float32).astype(dtype).astype(np.float64)
    return np.moveaxis((codes * scale).reshape(v.shape), -1, axis)


WIDE = False


def mx_kscale(k):
    if not WIDE:
        return np.ones(k)
    levels = np.array([18, -18])
    if k % 512:
        return np.exp2(np.random.permutation(np.resize(levels, k // 32))).repeat(32)
    a = np.empty((k // 512, 16))
    for p in range(k // 512):
        a[p, :8] = np.random.permutation(np.resize(levels, 8))
        for g in range(8):
            far = levels[np.abs(levels - a[p, g]) >= 10]
            a[p, g + 8] = far[np.random.randint(len(far))]
    return np.exp2(a.ravel()).repeat(32)


BF16 = ml_dtypes.bfloat16


def bf(x):
    return np.asarray(x, np.float32).astype(BF16)


def f64(x):
    return np.asarray(x).astype(np.float64)


B, S, D, F = 4, 256, 512, 2048
T = B * S
EPS = 1e-5
NTERMS = 150


def erf(a):
    a = np.clip(a, -6.0, 6.0)
    aa = 2.0 * a * a
    term = a.copy()
    tot = a.copy()
    for n in range(1, NTERMS):
        term = term * aa / (2.0 * n + 1.0)
        tot = tot + term
    return 2.0 / np.sqrt(np.pi) * np.exp(-a * a) * tot


def gelu(v):
    return 0.5 * v * (1.0 + erf(v / np.sqrt(2.0)))


def gelu_grad(v):
    return 0.5 * (1.0 + erf(v / np.sqrt(2.0))) + v * np.exp(-0.5 * v * v) / np.sqrt(2.0 * np.pi)


def forward_parts(attn_out, x, w_proj, b_proj, g2, beta2, w_fc1, b_fc1):
    proj = f64(attn_out) @ f64(w_proj) + f64(b_proj)
    x_mid = f64(x) + proj
    mu = x_mid.mean(-1, keepdims=True)
    var = np.square(x_mid - mu).mean(-1, keepdims=True)
    rstd = 1.0 / np.sqrt(var + EPS)
    h = (x_mid - mu) * rstd * f64(g2) + f64(beta2)
    z = h @ f64(w_fc1) + f64(b_fc1)
    return proj, np.concatenate([mu, rstd], -1), z, x_mid


def setup_inputs():
    u = mx_kscale(F)
    s = np.maximum(mx_kscale(T), 1.0).reshape(B, S, 1)
    attn_out = bf(0.25 * np.random.standard_normal((B, S, D)))
    x0 = bf(np.random.standard_normal((B, S, D)) * (0.5 + np.random.random((B, S, 1))) + 0.5 * np.random.standard_normal((B, S, 1)))
    w_proj = bf(2.0 * np.random.standard_normal((D, D)) / np.sqrt(D))
    b_proj = bf(0.1 * np.random.standard_normal(D))
    g2 = bf(1.0 + 0.1 * np.random.standard_normal(D))
    beta2 = bf(0.1 * np.random.standard_normal(D))
    w0 = bf(np.random.standard_normal((D, F)) / np.sqrt(D))
    b_fc1 = bf(0.1 * np.random.standard_normal(F))
    grad_0 = bf(np.random.standard_normal((B, S, D)) * np.exp2(np.random.randint(-6, 1, (B, S, 1))))
    grad_1 = bf(np.random.standard_normal((B, S, F)) * np.exp2(np.random.randint(-6, 1, (B, S, 1))) / s * u)
    proj, stats, z, x_mid = forward_parts(attn_out, x0, w_proj, b_proj, g2, beta2, w0, b_fc1)
    return {"attn_out": attn_out,
            "x": bf(f64(x0) * s),
            "w_proj": w_proj,
            "b_proj": b_proj,
            "g2": g2,
            "beta2": beta2,
            "w_fc1": bf(f64(w0) / u),
            "b_fc1": b_fc1,
            "proj": np.asarray(proj, np.float32),
            "stats": np.asarray(stats, np.float32),
            "z": np.asarray(z, np.float32),
            "grad_0": grad_0,
            "grad_1": grad_1}


def reference(attn_out, x, w_proj, b_proj, g2, beta2, w_fc1, b_fc1, proj, stats, z, grad_0, grad_1):
    st = f64(stats).reshape(T, 2)
    mu, rstd = st[:, 0:1], st[:, 1:2]
    gain = f64(g2)
    xhat = ((f64(x) + f64(proj)).reshape(T, D) - mu) * rstd
    h = xhat * gain + f64(beta2)
    dz = (f64(grad_1) * gelu_grad(f64(z))).reshape(T, F)
    dh = mxq(dz, 1, "e5m2") @ mxq(f64(w_fc1), 1, "e4m3").T
    dw_fc1 = mxq(h, 0, "e4m3").T @ mxq(dz, 0, "e5m2")
    dn = dh * gain
    back = rstd * (dn - dn.mean(-1, keepdims=True) - xhat * (dn * xhat).mean(-1, keepdims=True))
    dx = f64(grad_0) + back.reshape(B, S, D)
    return dx, dw_fc1

@@ -1,0 +1,457 @@
+from contextlib import ExitStack
+
+import concourse.mybir as mybir
+from concourse.masks import make_identity
+
+B, S, D, F = 4, 256, 512, 2048
+T = B * S
+FLOPS = 2 * 2 * T * D * F
+BYTES = 25176064
+
+F32 = mybir.dt.float32
+BF16 = mybir.dt.bfloat16
+U32 = mybir.dt.uint32
+U8 = mybir.dt.uint8
+E4 = mybir.dt.float8_e4m3fn_x4
+E5 = mybir.dt.float8_e5m2_x4
+ALU = mybir.AluOpType
+ACT = mybir.ActivationFunctionType
+
+P = 128
+J = 4
+NG = 2
+NC = 4
+CW = 512
+NB = 4
+H = 2.0 ** -7
+Z_MAX = 7.0
+Z_MIN = -30.0
+
+
+def tile_flashinferblock_pb_v_kernel(
+    tc, attn_out, x, w_proj, b_proj, g2, beta2, w_fc1, b_fc1, proj, stats, z, grad_0, grad_1, out_0, out_1
+):
+    nc = tc.nc
+
+    def tok(ap):
+        return ap.flatten_outer_dims().rearrange("(g p j) f -> g p j f", g=NG, j=J)
+
+    zv, gv, xv, pv, g0v, ov = tok(z), tok(grad_1), tok(x), tok(proj), tok(grad_0), tok(out_0)
+    sv = stats.flatten_outer_dims().rearrange("(g p j) s -> p g j s", g=NG, j=J)
+    wv = w_fc1.rearrange("(a p) f -> p a f", p=P)
+    o1v = out_1.rearrange("(a p) f -> a p f", p=P)
+
+    with ExitStack() as ctx:
+        keep = ctx.enter_context(tc.tile_pool(name="keep", bufs=1))
+        st8 = ctx.enter_context(tc.tile_pool(name="st8", bufs=7))
+        st4 = ctx.enter_context(tc.tile_pool(name="st4", bufs=6))
+        b4 = ctx.enter_context(tc.tile_pool(name="b4", bufs=5))
+        work = ctx.enter_context(tc.tile_pool(name="work", bufs=2))
+        work3 = ctx.enter_context(tc.tile_pool(name="work3", bufs=3))
+        psum = ctx.enter_context(tc.psum_pool(name="psum", bufs=2))
+
+        ident = keep.tile([P, P], F32, name="ident")
+        make_identity(nc, ident[:])
+        warm = keep.tile([P, 1], F32, name="warm")
+        nc.vector.memset(warm[:], 0.0)
+        nc.scalar.activation(out=warm[:], in_=warm[:], func=ACT.Gelu)
+
+        st = keep.tile([P, NG, J, 2], F32, name="st")
+        g2b = keep.tile([P, D], BF16, name="g2b")
+        b2b = keep.tile([P, D], BF16, name="b2b")
+        xhat = keep.tile([P, NG, J, D], F32, name="xhat")
+        hcodes = keep.tile([P, NG, D], U32, name="hcodes", align_bytes=64)
+        hscale = keep.tile([P, NG, D], U8, name="hscale", align_bytes=64)
+        wcodes = keep.tile([P, NC, D], U32, name="wcodes", align_bytes=64)
+        wscale = keep.tile([P, NC, D], U8, name="wscale", align_bytes=64)
+        fcodes, fscale, tcodes, tscale = {}, {}, {}, {}
+        zt, gt, xt, pt, g0t, wt = {}, {}, {}, {}, {}, {}
+        for g in range(NG):
+            for c in range(NC):
+                fcodes[g, c] = keep.tile([P, CW], U32, name="fc%d%d" % (g, c), align_bytes=64)
+                fscale[g, c] = keep.tile([P, CW], U8, name="fs%d%d" % (g, c), align_bytes=64)
+        for c in range(NC):
+            tcodes[0, c] = keep.tile([P, CW], U32, name="tc%d" % c, align_bytes=64)
+            tscale[0, c] = keep.tile([P, CW], U8, name="ts%d" % c, align_bytes=64)
+
+        ctx.enter_context(tc.manual_schedule())
+
+        def load_z(g, c, pieces):
+            a = st8.tile([P, J, CW], F32, name="zc", tag="s8")
+            w = CW // pieces
+            for i in range(pieces):
+                nc.sync.dma_start(
+                    out=a[:, :, i * w : (i + 1) * w], in_=zv[g, :, :, c * CW + i * w : c * CW + (i + 1) * w]
+                )
+            zt[g, c] = a
+
+        def load_g(g, c):
+            b = st4.tile([P, J, CW], BF16, name="gc", tag="s4")
+            nc.sync.dma_start(out=b[:], in_=gv[g, :, :, c * CW : (c + 1) * CW])
+            gt[g, c] = b
+
+        def load_w(k):
+            a = st8.tile([P, 2, F], BF16, name="wr", tag="s8")
+            nc.sync.dma_start(out=a[:], in_=wv[:, 2 * k : 2 * k + 2, :])
+            wt[k] = a
+
+        def load_x(g):
+            a = st4.tile([P, J, D], BF16, name="xr", tag="s4")
+            nc.sync.dma_start(out=a[:], in_=xv[g])
+            b = st8.tile([P, J, D], F32, name="pr", tag="s8")
+            nc.sync.dma_start(out=b[:], in_=pv[g])
+            xt[g] = a
+            pt[g] = b
+
+        def load_g0(g):
+            a = st4.tile([P, J, D], BF16, name="g0", tag="s4")
+            nc.sync.dma_start(out=a[:], in_=g0v[g])
+            g0t[g] = a
+
+        def load_vec():
+            nc.sync.dma_start(out=g2b[:], in_=g2.partition_broadcast(P))
+            nc.sync.dma_start(out=b2b[:], in_=beta2.partition_broadcast(P))
+
+        gel, e8, nn, zp, dp, dzc, ftp, dzf = {}, {}, {}, {}, {}, {}, {}, {}
+
+        def gcb(s):
+            return s // 16, (s // 4) % 4, s % 4
+
+        def clamp(s):
+            g, c, b = gcb(s)
+            a = zt[g, c][:, :, b * P : (b + 1) * P]
+            nc.vector.tensor_scalar(out=a, in0=a, scalar1=Z_MAX, scalar2=Z_MIN, op0=ALU.min, op1=ALU.max)
+
+        def z_transposes(s):
+            g, c, b = gcb(s)
+            zp[s] = psum.tile([P, J, P], F32, name="zp", tag="zp")
+            for j in range(J):
+                nc.tensor.transpose(zp[s][:, j, :], zt[g, c][:, j, b * P : (b + 1) * P], ident[:])
+
+        def gelus(s):
+            src = zp[s][:].rearrange("p j f -> p (j f)")
+            for k, off in ((2, H), (1, -H), (3, 2.0 * H), (0, -2.0 * H)):
+                t = work3.tile([P, J, P], F32, name="ge%d" % k, tag="ge%d" % k)
+                nc.scalar.activation(out=t[:].rearrange("p j f -> p (j f)"), in_=src, func=ACT.Gelu, bias=off)
+                gel[s, k] = t
+
+        def eight(s):
+            e8[s] = work3.tile([P, J, P], F32, name="e8", tag="e8")
+            nc.gpsimd.tensor_scalar(
+                out=e8[s][:], in0=gel[s, 2][:], scalar1=8.0, scalar2=0.0, op0=ALU.mult, op1=ALU.add
+            )
+
+        def negative(s):
+            nn[s] = work3.tile([P, J, P], F32, name="nn", tag="nn")
+            nc.vector.scalar_tensor_tensor(
+                out=nn[s][:].rearrange("p j f -> p (j f)"),
+                in0=gel[s, 1][:].rearrange("p j f -> p (j f)"),
+                scalar=-8.0,
+                in1=gel[s, 3][:].rearrange("p j f -> p (j f)"),
+                op0=ALU.mult,
+                op1=ALU.subtract,
+            )
+
+        def sums(s):
+            dp[s] = psum.tile([P, J, P], F32, name="dp", tag="dp")
+            for j in range(J):
+                terms = (gel[s, 0], nn[s], e8[s])
+                for i, t in enumerate(terms):
+                    nc.tensor.matmul(
+                        dp[s][:, j, :], lhsT=t[:, j, :], rhs=ident[:], is_transpose=True, start=(i == 0), stop=(i == 2)
+                    )
+
+        def dz(s):
+            g, c, b = gcb(s)
+            if b == 0:
+                dzc[g, c] = b4.tile([P, CW, J], BF16, name="dzc", tag="b4", align_bytes=64)
+            nc.vector.scalar_tensor_tensor(
+                out=dzc[g, c][:, b * P : (b + 1) * P, :],
+                in0=dp[s][:].rearrange("p j f -> p f j"),
+                scalar=1.0 / (12.0 * H),
+                in1=gt[g, c][:, :, b * P : (b + 1) * P].rearrange("p j f -> p f j"),
+                op0=ALU.mult,
+                op1=ALU.mult,
+            )
+
+        def quant_tok(g, c):
+            if g == 1:
+                tcodes[g, c] = work.tile([P, CW], U32, name="tc1", tag="tc1", align_bytes=64)
+                tscale[g, c] = work.tile([P, CW], U8, name="ts1", tag="ts1", align_bytes=64)
+            nc.vector.quantize_mx(
+                out=tcodes[g, c][:].bitcast(E5), scales=tscale[g, c][:], in_=dzc[g, c][:].rearrange("p f j -> p (f j)")
+            )
+
+        def f_transposes(g, c):
+            words = dzc[g, c][:].rearrange("p f j -> p (f j)").bitcast(F32)
+            for u in range(2):
+                tp = psum.tile([P, 4, P], F32, name="ftp", tag="ftp")
+                for t in range(4):
+                    nc.tensor.transpose(tp[:, t, :], words[:, 2 * t + u : 2 * CW : 8], ident[:])
+                ftp[g, c, u] = tp
+
+        def f_copy(g, c, u, scalar):
+            if u == 0:
+                dzf[g, c] = b4.tile([P, 2, 2, P, 4], BF16, name="dzf", tag="b4", align_bytes=64)
+            src = ftp[g, c, u][:].rearrange("p t r -> p (t r)").bitcast(BF16)
+            src = src.rearrange("p (t r e) -> p e r t", t=4, e=2)
+            if scalar:
+                nc.scalar.copy(out=dzf[g, c][:, u], in_=src)
+            else:
+                nc.vector.tensor_copy(out=dzf[g, c][:, u], in_=src)
+
+        def quant_f(g, c):
+            nc.vector.quantize_mx(
+                out=fcodes[g, c][:].bitcast(E5),
+                scales=fscale[g, c][:],
+                in_=dzf[g, c][:].rearrange("p u e r t -> p (u e r t)"),
+            )
+
+        wg = {}
+        wtp = {}
+
+        def w_turn(c, k):
+            if k == 0:
+                wg[c] = b4.tile([P, 4, P, 4], BF16, name="wg", tag="b4", align_bytes=64)
+            tp = psum.tile([P, 2, 2, P], F32, name="wtp", tag="ftp")
+            for a in range(2):
+                words = wt[k][:, a, :].bitcast(F32)
+                for u in range(2):
+                    nc.tensor.transpose(tp[:, a, u, :], words[:, 256 * c + u : 256 * (c + 1) : 2], ident[:])
+            wtp[c, k] = tp
+
+        def w_copy(c, k):
+            dst = wg[c][:].rearrange("p a r t -> p (a r t)").bitcast(F32)
+            dst = dst.rearrange("p (a r u) -> p a r u", a=4, u=2)
+            nc.vector.tensor_copy(out=dst[:, 2 * k : 2 * k + 2], in_=wtp[c, k][:].rearrange("p a u r -> p a r u"))
+
+        def w_quant(c):
+            nc.vector.quantize_mx(
+                out=wcodes[:, c, :].bitcast(E4), scales=wscale[:, c, :], in_=wg[c][:].rearrange("p a r t -> p (a r t)")
+            )
+
+        hg, hb = {}, {}
+
+        def h_sum(g, j):
+            nc.gpsimd.tensor_tensor(out=pt[g][:, j, :], in0=pt[g][:, j, :], in1=xt[g][:, j, :], op=ALU.add)
+
+        def h_norm(g, j):
+            nc.vector.tensor_scalar(
+                out=xhat[:, g, j, :],
+                in0=pt[g][:, j, :],
+                scalar1=st[:, g, j, 0:1],
+                scalar2=st[:, g, j, 1:2],
+                op0=ALU.subtract,
+                op1=ALU.mult,
+            )
+
+        def h_gain(g, k):
+            if k == 0:
+                hg[g] = st8.tile([P, J, D], F32, name="hg", tag="s8")
+            nc.vector.tensor_tensor(
+                out=hg[g][:, 2 * k : 2 * k + 2],
+                in0=xhat[:, g, 2 * k : 2 * k + 2],
+                in1=g2b[:].unsqueeze(1).to_broadcast([P, 2, D]),
+                op=ALU.mult,
+            )
+
+        def h_shift(g, k):
+            if k == 0:
+                hb[g] = b4.tile([P, D, J], BF16, name="hb", tag="b4", align_bytes=64)
+            w = slice(k * (D // 2), (k + 1) * (D // 2))
+            nc.vector.tensor_tensor(
+                out=hb[g][:, w],
+                in0=hg[g][:, :, w].rearrange("p j d -> p d j"),
+                in1=b2b[:, w].unsqueeze(2).to_broadcast([P, D // 2, J]),
+                op=ALU.add,
+            )
+
+        def h_quant(g):
+            nc.vector.quantize_mx(
+                out=hcodes[:, g, :].bitcast(E4), scales=hscale[:, g, :], in_=hb[g][:].rearrange("p d j -> p (d j)")
+            )
+
+        def weight_grad(c, a):
+            acc = psum.tile([P, CW], F32, name="acc", tag="mm")
+            for g in range(NG):
+                nc.tensor.matmul_mx(
+                    out=acc[:],
+                    lhsT=hcodes[:, g, a * P : (a + 1) * P].bitcast(E4),
+                    lhsT_scale=hscale[:, g, a * P : (a + 1) * P],
+                    rhs=tcodes[g, c][:].bitcast(E5),
+                    rhs_scale=tscale[g, c][:],
+                    start=(g == 0),
+                    stop=(g == NG - 1),
+                )
+            res = work3.tile([P, CW], F32, name="res", tag="res")
+            nc.scalar.copy(out=res[:], in_=acc[:])
+            nc.sync.dma_start(out=o1v[a, :, c * CW : (c + 1) * CW], in_=res[:])
+
+        dh, s12, dn, qq = {}, {}, {}, {}
+
+        def dg_mm(g, j, cs, tag):
+            if cs[0] == 0:
+                dh[g, j] = psum.tile([P, D], F32, name="dh", tag=tag)
+            for c in cs:
+                nc.tensor.matmul_mx(
+                    out=dh[g, j][:],
+                    lhsT=fcodes[g, c][:, j * P : (j + 1) * P].bitcast(E5),
+                    lhsT_scale=fscale[g, c][:, j * P : (j + 1) * P],
+                    rhs=wcodes[:, c, :].bitcast(E4),
+                    rhs_scale=wscale[:, c, :],
+                    start=(c == 0),
+                    stop=(c == NC - 1),
+                )
+
+        def dg_dn(g, j):
+            s12[g, j] = work.tile([P, 16], F32, name="s12", tag="s12")
+            dn[g, j] = work3.tile([P, D], F32, name="dn", tag="dn")
+            nc.vector.scalar_tensor_tensor(
+                out=dn[g, j][:],
+                in0=dh[g, j][:],
+                scalar=1.0,
+                in1=g2b[:],
+                op0=ALU.mult,
+                op1=ALU.mult,
+                accum_out=s12[g, j][:, 0:1],
+            )
+
+        def dg_dot(g, j):
+            junk = work.tile([P, D], F32, name="junk", tag="r")
+            nc.vector.scalar_tensor_tensor(
+                out=junk[:],
+                in0=dn[g, j][:],
+                scalar=1.0,
+                in1=xhat[:, g, j, :],
+                op0=ALU.mult,
+                op1=ALU.mult,
+                accum_out=s12[g, j][:, 1:2],
+            )
+            nc.vector.tensor_scalar(
+                out=s12[g, j][:, 8:10],
+                in0=s12[g, j][:, 0:2],
+                scalar1=-1.0 / D,
+                scalar2=st[:, g, j, 1:2],
+                op0=ALU.mult,
+                op1=ALU.mult,
+            )
+
+        def dg_q(g, j):
+            qq[g, j] = work.tile([P, D], F32, name="q", tag="q")
+            nc.scalar.activation(
+                out=qq[g, j][:],
+                in_=xhat[:, g, j, :],
+                func=ACT.Identity,
+                scale=s12[g, j][:, 9:10],
+                bias=s12[g, j][:, 8:9],
+            )
+
+        def dg_out(g, j):
+            r = work.tile([P, D], F32, name="r", tag="r")
+            nc.vector.scalar_tensor_tensor(
+                out=r[:], in0=dn[g, j][:], scalar=st[:, g, j, 1:2], in1=qq[g, j][:], op0=ALU.mult, op1=ALU.add
+            )
+            o = work.tile([P, D], F32, name="o", tag="o")
+            nc.gpsimd.tensor_tensor(out=o[:], in0=r[:], in1=g0t[g][:, j, :], op=ALU.add)
+            nc.sync.dma_start(out=ov[g, :, j, :], in_=o[:])
+
+        n = NG * NC * NB
+        pre = [[] for w in range(n + 12)]
+        post = [[] for w in range(n + 12)]
+        for k in range(8):
+            g, c = k // 4, k % 4
+            w = 4 * k + 6
+            pre[w].append((f_transposes, (g, c)))
+            post[w].append((f_copy, (g, c, 0, g == 0)))
+            post[w].append((quant_tok, (g, c)))
+            post[w + 1].append((f_copy, (g, c, 1, g == 0 or k == 7)))
+            if k < 7:
+                post[w + 2].append((quant_f, (g, c)))
+            if k >= 2:
+                post[4 * (k - 2) + 1].append((load_z, (g, c, 1)))
+                post[4 * (k - 2) + 2].append((load_g, (g, c)))
+        post[2].append((load_x, (0,)))
+        post[6].append((load_vec, ()))
+        post[10].append((load_x, (1,)))
+        post[15].append((load_g0, (0,)))
+        post[23].append((load_g0, (1,)))
+        for i in range(8):
+            c, k = i // 2, i % 2
+            post[3 + i].append((w_turn, (c, k)))
+            post[4 + i].append((w_copy, (c, k)))
+            if k == 1:
+                post[5 + i].append((w_quant, (c,)))
+        for g, w in ((0, 8), (1, 14)):
+            for j in range(J):
+                post[w - 1 + j].append((h_sum, (g, j)))
+                post[w + j].append((h_norm, (g, j)))
+            post[w + 2].append((h_gain, (g, 0)))
+            post[w + 4].append((h_gain, (g, 1)))
+            post[w + 5].append((h_shift, (g, 0)))
+            post[w + 5].append((h_shift, (g, 1)))
+            post[w + 6].append((h_quant, (g,)))
+        for j in range(J):
+            w = 21 + j
+            post[w].append((dg_mm, (0, j, (0, 1, 2, 3), "mm")))
+            post[w].append((dg_dn, (0, j)))
+            post[w + 1].append((dg_dot, (0, j)))
+            post[w + 2].append((dg_q, (0, j)))
+            post[w + 3].append((dg_out, (0, j)))
+        for c in range(NC):
+            for a in range(4):
+                w = 4 * c + 23 + a
+                if c == 3:
+                    w = 35
+                post[w].append((weight_grad, (c, a)))
+
+        nc.sync.dma_start(out=st[:], in_=sv)
+        load_z(0, 0, 4)
+        load_g(0, 0)
+        load_z(0, 1, 1)
+        load_w(0)
+        load_w(1)
+        load_g(0, 1)
+        clamp(0)
+        clamp(1)
+        z_transposes(0)
+        for s in range(n + 4):
+            for f, args in pre[s]:
+                f(*args)
+            if s + 1 < n:
+                z_transposes(s + 1)
+            if s < n:
+                gelus(s)
+                eight(s)
+            if 1 <= s <= n:
+                negative(s - 1)
+                sums(s - 1)
+            if 2 <= s <= n + 1:
+                dz(s - 2)
+            if s + 2 < n:
+                clamp(s + 2)
+            for f, args in post[s]:
+                f(*args)
+            if s == n:
+                dg_mm(1, 0, (0, 1, 2), "zp")
+                dg_mm(1, 1, (0, 1, 2), "zp")
+        quant_f(1, 3)
+        dg_mm(1, 0, (3,), "zp")
+        dg_mm(1, 1, (3,), "zp")
+        dg_mm(1, 2, (0, 1, 2, 3), "dp")
+        dg_mm(1, 3, (0, 1, 2, 3), "dp")
+        dg_dn(1, 0)
+        dg_dn(1, 1)
+        dg_dot(1, 0)
+        dg_dot(1, 1)
+        dg_q(1, 0)
+        dg_q(1, 1)
+        dg_dn(1, 2)
+        dg_out(1, 0)
+        dg_dot(1, 2)
+        dg_out(1, 1)
+        dg_q(1, 2)
+        dg_dn(1, 3)
+        dg_dot(1, 3)
+        dg_q(1, 3)
+        dg_out(1, 2)
+        dg_out(1, 3)

@@ -23,7 +23,34 @@ NG = 2
 NC = 4
 CW = 512
 NB = 4
-H = 2.0 ** -7
+REP = 2
+ORDER = ((0, 0), (0, 1), (1, 0), (0, 2), (0, 3), (1, 1), (1, 2), (1, 3))
+PE_LATE = 0
+ZA = 1
+R_ZP = 2
+R_FT = 2
+R_MM = 2
+FT = (6, 7)
+FC = (6, 7)
+FC_ENG = "SSSSSVVVVVVSSS"
+QT = 7
+QF = 8
+H_AT = (2, 8)
+H_ENG = "VV"
+W_AT = 10
+W_STEP = 1
+W_ENG = "S"
+DG_AT = 25
+DG_STEP = 1
+O_ENG = "V"
+WG_AT = (19, 28, 33)
+WG_STEP = (1, 1, 1)
+WO_ENG = "SVSSSSSVSSSS"
+WC_LAG = 0
+WO_LAG = 1
+LW = (8, 10)
+H1 = 2.0 ** -6.5
+H2 = H1 * REP ** (1.0 / 3.0)
 Z_MAX = 7.0
 Z_MIN = -30.0
 
@@ -43,12 +70,16 @@ def tile_flashinferblock_pb_v_kernel(
 
     with ExitStack() as ctx:
         keep = ctx.enter_context(tc.tile_pool(name="keep", bufs=1))
-        st8 = ctx.enter_context(tc.tile_pool(name="st8", bufs=7))
+        st8 = ctx.enter_context(tc.tile_pool(name="st8", bufs=6))
         st4 = ctx.enter_context(tc.tile_pool(name="st4", bufs=6))
-        b4 = ctx.enter_context(tc.tile_pool(name="b4", bufs=5))
+        b4 = ctx.enter_context(tc.tile_pool(name="b4", bufs=6))
         work = ctx.enter_context(tc.tile_pool(name="work", bufs=2))
         work3 = ctx.enter_context(tc.tile_pool(name="work3", bufs=3))
+        work4 = ctx.enter_context(tc.tile_pool(name="work4", bufs=4))
         psum = ctx.enter_context(tc.psum_pool(name="psum", bufs=2))
+        psum3 = ctx.enter_context(tc.psum_pool(name="psum3", bufs=R_ZP))
+        psum1 = ctx.enter_context(tc.psum_pool(name="psum1", bufs=R_FT))
+        psumm = ctx.enter_context(tc.psum_pool(name="psumm", bufs=R_MM))
 
         ident = keep.tile([P, P], F32, name="ident")
         make_identity(nc, ident[:])
@@ -60,6 +91,8 @@ def tile_flashinferblock_pb_v_kernel(
         g2b = keep.tile([P, D], BF16, name="g2b")
         b2b = keep.tile([P, D], BF16, name="b2b")
         xhat = keep.tile([P, NG, J, D], F32, name="xhat")
+        hg = keep.tile([P, NG, J, D], F32, name="hg")
+        rneg = keep.tile([P, NG, J], F32, name="rneg")
         hcodes = keep.tile([P, NG, D], U32, name="hcodes", align_bytes=64)
         hscale = keep.tile([P, NG, D], U8, name="hscale", align_bytes=64)
         wcodes = keep.tile([P, NC, D], U32, name="wcodes", align_bytes=64)
@@ -112,41 +145,44 @@ def tile_flashinferblock_pb_v_kernel(
             nc.sync.dma_start(out=g2b[:], in_=g2.partition_broadcast(P))
             nc.sync.dma_start(out=b2b[:], in_=beta2.partition_broadcast(P))
 
-        gel, e8, nn, zp, dp, dzc, ftp, dzf = {}, {}, {}, {}, {}, {}, {}, {}
+        gel, nn, zp, dp, dzc, ftp, dzf = {}, {}, {}, {}, {}, {}, {}
 
         def gcb(s):
-            return s // 16, (s // 4) % 4, s % 4
+            return ORDER[s // 4] + (s % 4,)
+
+        def part(s):
+            b = s % 4
+            if s // 4 < 7:
+                return slice(0, 4), slice(b * P, (b + 1) * P)
+            return slice(b // 2 * 2, b // 2 * 2 + 2), slice(b % 2 * 2 * P, (b % 2 * 2 + 2) * P)
 
         def clamp(s):
             g, c, b = gcb(s)
-            a = zt[g, c][:, :, b * P : (b + 1) * P]
+            js, fs = part(s)
+            a = zt[g, c][:, js, fs]
             nc.vector.tensor_scalar(out=a, in0=a, scalar1=Z_MAX, scalar2=Z_MIN, op0=ALU.min, op1=ALU.max)
 
         def z_transposes(s):
             g, c, b = gcb(s)
-            zp[s] = psum.tile([P, J, P], F32, name="zp", tag="zp")
-            for j in range(J):
-                nc.tensor.transpose(zp[s][:, j, :], zt[g, c][:, j, b * P : (b + 1) * P], ident[:])
+            zp[s] = psum3.tile([P, J, P], F32, name="zp", tag="zp")
+            js, fs = part(s)
+            blocks = [(j, f) for j in range(js.start, js.stop) for f in range(fs.start, fs.stop, P)]
+            for i, (j, f) in enumerate(blocks):
+                nc.tensor.transpose(zp[s][:, i, :], zt[g, c][:, j, f : f + P], ident[:])
 
         def gelus(s):
             src = zp[s][:].rearrange("p j f -> p (j f)")
-            for k, off in ((2, H), (1, -H), (3, 2.0 * H), (0, -2.0 * H)):
+            for k, off in ((1, -H1), (3, H2), (2, H1), (0, -H2)):
                 t = work3.tile([P, J, P], F32, name="ge%d" % k, tag="ge%d" % k)
                 nc.scalar.activation(out=t[:].rearrange("p j f -> p (j f)"), in_=src, func=ACT.Gelu, bias=off)
                 gel[s, k] = t
 
-        def eight(s):
-            e8[s] = work3.tile([P, J, P], F32, name="e8", tag="e8")
-            nc.gpsimd.tensor_scalar(
-                out=e8[s][:], in0=gel[s, 2][:], scalar1=8.0, scalar2=0.0, op0=ALU.mult, op1=ALU.add
-            )
-
         def negative(s):
-            nn[s] = work3.tile([P, J, P], F32, name="nn", tag="nn")
+            nn[s] = work.tile([P, J, P], F32, name="nn", tag="nn")
             nc.vector.scalar_tensor_tensor(
                 out=nn[s][:].rearrange("p j f -> p (j f)"),
                 in0=gel[s, 1][:].rearrange("p j f -> p (j f)"),
-                scalar=-8.0,
+                scalar=-float(REP),
                 in1=gel[s, 3][:].rearrange("p j f -> p (j f)"),
                 op0=ALU.mult,
                 op1=ALU.subtract,
@@ -155,21 +191,22 @@ def tile_flashinferblock_pb_v_kernel(
         def sums(s):
             dp[s] = psum.tile([P, J, P], F32, name="dp", tag="dp")
             for j in range(J):
-                terms = (gel[s, 0], nn[s], e8[s])
+                terms = [gel[s, 2]] * REP + [gel[s, 0], nn[s]]
                 for i, t in enumerate(terms):
                     nc.tensor.matmul(
-                        dp[s][:, j, :], lhsT=t[:, j, :], rhs=ident[:], is_transpose=True, start=(i == 0), stop=(i == 2)
+                        dp[s][:, j, :], lhsT=t[:, j, :], rhs=ident[:], is_transpose=True, start=(i == 0), stop=(i == REP + 1)
                     )
 
         def dz(s):
             g, c, b = gcb(s)
             if b == 0:
                 dzc[g, c] = b4.tile([P, CW, J], BF16, name="dzc", tag="b4", align_bytes=64)
+            js, fs = part(s)
             nc.vector.scalar_tensor_tensor(
-                out=dzc[g, c][:, b * P : (b + 1) * P, :],
-                in0=dp[s][:].rearrange("p j f -> p f j"),
-                scalar=1.0 / (12.0 * H),
-                in1=gt[g, c][:, :, b * P : (b + 1) * P].rearrange("p j f -> p f j"),
+                out=dzc[g, c][:, fs, js],
+                in0=dp[s][:].rearrange("p i f -> p (i f)").rearrange("p (j f) -> p f j", j=js.stop - js.start),
+                scalar=0.5 / (REP * H1 - H2),
+                in1=gt[g, c][:, js, fs].rearrange("p j f -> p f j"),
                 op0=ALU.mult,
                 op1=ALU.mult,
             )
@@ -182,16 +219,18 @@ def tile_flashinferblock_pb_v_kernel(
                 out=tcodes[g, c][:].bitcast(E5), scales=tscale[g, c][:], in_=dzc[g, c][:].rearrange("p f j -> p (f j)")
             )
 
-        def f_transposes(g, c):
+        def f_transposes(g, c, u):
             words = dzc[g, c][:].rearrange("p f j -> p (f j)").bitcast(F32)
-            for u in range(2):
-                tp = psum.tile([P, 4, P], F32, name="ftp", tag="ftp")
-                for t in range(4):
-                    nc.tensor.transpose(tp[:, t, :], words[:, 2 * t + u : 2 * CW : 8], ident[:])
-                ftp[g, c, u] = tp
+            if (g, c, u) == (1, 3, 1):
+                tp = psum.tile([P, 4, P], F32, name="ftp2", tag="dp")
+            else:
+                tp = psum1.tile([P, 4, P], F32, name="ftp", tag="ftp")
+            for t in range(4):
+                nc.tensor.transpose(tp[:, t, :], words[:, 2 * t + u : 2 * CW : 8], ident[:])
+            ftp[g, c, u] = tp
 
         def f_copy(g, c, u, scalar):
-            if u == 0:
+            if (g, c) not in dzf:
                 dzf[g, c] = b4.tile([P, 2, 2, P, 4], BF16, name="dzf", tag="b4", align_bytes=64)
             src = ftp[g, c, u][:].rearrange("p t r -> p (t r)").bitcast(BF16)
             src = src.rearrange("p (t r e) -> p e r t", t=4, e=2)
@@ -200,11 +239,11 @@ def tile_flashinferblock_pb_v_kernel(
             else:
                 nc.vector.tensor_copy(out=dzf[g, c][:, u], in_=src)
 
-        def quant_f(g, c):
+        def quant_f(g, c, lo, hi):
             nc.vector.quantize_mx(
-                out=fcodes[g, c][:].bitcast(E5),
-                scales=fscale[g, c][:],
-                in_=dzf[g, c][:].rearrange("p u e r t -> p (u e r t)"),
+                out=fcodes[g, c][:, 2 * P * lo : 2 * P * hi].bitcast(E5),
+                scales=fscale[g, c][:, 2 * P * lo : 2 * P * hi],
+                in_=dzf[g, c][:, lo:hi].rearrange("p u e r t -> p (u e r t)"),
             )
 
         wg = {}
@@ -213,27 +252,28 @@ def tile_flashinferblock_pb_v_kernel(
         def w_turn(c, k):
             if k == 0:
                 wg[c] = b4.tile([P, 4, P, 4], BF16, name="wg", tag="b4", align_bytes=64)
-            tp = psum.tile([P, 2, 2, P], F32, name="wtp", tag="ftp")
+            tp = psum1.tile([P, 2, 2, P], F32, name="wtp", tag="ftp")
             for a in range(2):
                 words = wt[k][:, a, :].bitcast(F32)
                 for u in range(2):
                     nc.tensor.transpose(tp[:, a, u, :], words[:, 256 * c + u : 256 * (c + 1) : 2], ident[:])
             wtp[c, k] = tp
 
-        def w_copy(c, k):
+        def w_copy(c, k, scalar):
             dst = wg[c][:].rearrange("p a r t -> p (a r t)").bitcast(F32)
             dst = dst.rearrange("p (a r u) -> p a r u", a=4, u=2)
-            nc.vector.tensor_copy(out=dst[:, 2 * k : 2 * k + 2], in_=wtp[c, k][:].rearrange("p a u r -> p a r u"))
+            copy = nc.scalar.copy if scalar else nc.vector.tensor_copy
+            copy(out=dst[:, 2 * k : 2 * k + 2], in_=wtp[c, k][:].rearrange("p a u r -> p a r u"))
 
         def w_quant(c):
             nc.vector.quantize_mx(
                 out=wcodes[:, c, :].bitcast(E4), scales=wscale[:, c, :], in_=wg[c][:].rearrange("p a r t -> p (a r t)")
             )
 
-        hg, hb = {}, {}
+        hb = {}
 
-        def h_sum(g, j):
-            nc.gpsimd.tensor_tensor(out=pt[g][:, j, :], in0=pt[g][:, j, :], in1=xt[g][:, j, :], op=ALU.add)
+        def h_sum(g, j, eng):
+            eng.tensor_tensor(out=pt[g][:, j, :], in0=pt[g][:, j, :], in1=xt[g][:, j, :], op=ALU.add)
 
         def h_norm(g, j):
             nc.vector.tensor_scalar(
@@ -246,10 +286,8 @@ def tile_flashinferblock_pb_v_kernel(
             )
 
         def h_gain(g, k):
-            if k == 0:
-                hg[g] = st8.tile([P, J, D], F32, name="hg", tag="s8")
             nc.vector.tensor_tensor(
-                out=hg[g][:, 2 * k : 2 * k + 2],
+                out=hg[:, g, 2 * k : 2 * k + 2],
                 in0=xhat[:, g, 2 * k : 2 * k + 2],
                 in1=g2b[:].unsqueeze(1).to_broadcast([P, 2, D]),
                 op=ALU.mult,
@@ -261,7 +299,7 @@ def tile_flashinferblock_pb_v_kernel(
             w = slice(k * (D // 2), (k + 1) * (D // 2))
             nc.vector.tensor_tensor(
                 out=hb[g][:, w],
-                in0=hg[g][:, :, w].rearrange("p j d -> p d j"),
+                in0=hg[:, g, :, w].rearrange("p j d -> p d j"),
                 in1=b2b[:, w].unsqueeze(2).to_broadcast([P, D // 2, J]),
                 op=ALU.add,
             )
@@ -271,8 +309,10 @@ def tile_flashinferblock_pb_v_kernel(
                 out=hcodes[:, g, :].bitcast(E4), scales=hscale[:, g, :], in_=hb[g][:].rearrange("p d j -> p (d j)")
             )
 
+        wacc = {}
+
         def weight_grad(c, a):
-            acc = psum.tile([P, CW], F32, name="acc", tag="mm")
+            acc = psumm.tile([P, CW], F32, name="acc", tag="mm")
             for g in range(NG):
                 nc.tensor.matmul_mx(
                     out=acc[:],
@@ -283,15 +323,20 @@ def tile_flashinferblock_pb_v_kernel(
                     start=(g == 0),
                     stop=(g == NG - 1),
                 )
-            res = work3.tile([P, CW], F32, name="res", tag="res")
-            nc.scalar.copy(out=res[:], in_=acc[:])
+            wacc[c, a] = acc
+
+        def weight_out(c, a, scalar):
+            acc = wacc[c, a]
+            res = work4.tile([P, CW], F32, name="res", tag="res")
+            copy = nc.scalar.copy if scalar else nc.vector.tensor_copy
+            copy(out=res[:], in_=acc[:])
             nc.sync.dma_start(out=o1v[a, :, c * CW : (c + 1) * CW], in_=res[:])
 
         dh, s12, dn, qq = {}, {}, {}, {}
 
         def dg_mm(g, j, cs, tag):
             if cs[0] == 0:
-                dh[g, j] = psum.tile([P, D], F32, name="dh", tag=tag)
+                dh[g, j] = {"zp": psum3, "dp": psum, "mm": psumm}[tag].tile([P, D], F32, name="dh", tag=tag)
             for c in cs:
                 nc.tensor.matmul_mx(
                     out=dh[g, j][:],
@@ -303,155 +348,195 @@ def tile_flashinferblock_pb_v_kernel(
                     stop=(c == NC - 1),
                 )
 
-        def dg_dn(g, j):
-            s12[g, j] = work.tile([P, 16], F32, name="s12", tag="s12")
+        def dg_read(g, j):
+            s12[g, j] = work3.tile([P, 8], F32, name="s12", tag="s12")
             dn[g, j] = work3.tile([P, D], F32, name="dn", tag="dn")
-            nc.vector.scalar_tensor_tensor(
-                out=dn[g, j][:],
-                in0=dh[g, j][:],
-                scalar=1.0,
-                in1=g2b[:],
-                op0=ALU.mult,
-                op1=ALU.mult,
-                accum_out=s12[g, j][:, 0:1],
-            )
-
-        def dg_dot(g, j):
-            junk = work.tile([P, D], F32, name="junk", tag="r")
-            nc.vector.scalar_tensor_tensor(
-                out=junk[:],
-                in0=dn[g, j][:],
-                scalar=1.0,
-                in1=xhat[:, g, j, :],
-                op0=ALU.mult,
-                op1=ALU.mult,
-                accum_out=s12[g, j][:, 1:2],
-            )
-            nc.vector.tensor_scalar(
-                out=s12[g, j][:, 8:10],
-                in0=s12[g, j][:, 0:2],
-                scalar1=-1.0 / D,
-                scalar2=st[:, g, j, 1:2],
-                op0=ALU.mult,
-                op1=ALU.mult,
-            )
+            junk = work.tile([P, D], F32, name="junk", tag="nn")
+            for i, (dst, row) in enumerate(((dn[g, j], g2b[:]), (junk, hg[:, g, j, :]))):
+                nc.vector.scalar_tensor_tensor(
+                    out=dst[:],
+                    in0=dh[g, j][:],
+                    scalar=rneg[:, g, j : j + 1],
+                    in1=row,
+                    op0=ALU.mult,
+                    op1=ALU.mult,
+                    accum_out=s12[g, j][:, i : i + 1],
+                )
 
         def dg_q(g, j):
-            qq[g, j] = work.tile([P, D], F32, name="q", tag="q")
+            qq[g, j] = work4.tile([P, D], F32, name="q", tag="q")
             nc.scalar.activation(
                 out=qq[g, j][:],
                 in_=xhat[:, g, j, :],
                 func=ACT.Identity,
-                scale=s12[g, j][:, 9:10],
-                bias=s12[g, j][:, 8:9],
+                scale=s12[g, j][:, 1:2],
+                bias=s12[g, j][:, 0:1],
             )
 
-        def dg_out(g, j):
-            r = work.tile([P, D], F32, name="r", tag="r")
+        def dg_r(g, j):
             nc.vector.scalar_tensor_tensor(
-                out=r[:], in0=dn[g, j][:], scalar=st[:, g, j, 1:2], in1=qq[g, j][:], op0=ALU.mult, op1=ALU.add
+                out=qq[g, j][:], in0=dn[g, j][:], scalar=-float(D), in1=qq[g, j][:], op0=ALU.mult, op1=ALU.add
             )
-            o = work.tile([P, D], F32, name="o", tag="o")
-            nc.gpsimd.tensor_tensor(out=o[:], in0=r[:], in1=g0t[g][:, j, :], op=ALU.add)
+
+        def dg_out(g, j, vector):
+            eng = nc.vector if vector else nc.gpsimd
+            o = work4.tile([P, D], F32, name="o", tag="q")
+            eng.tensor_tensor(out=o[:], in0=qq[g, j][:], in1=g0t[g][:, j, :], op=ALU.add)
             nc.sync.dma_start(out=ov[g, :, j, :], in_=o[:])
 
         n = NG * NC * NB
-        pre = [[] for w in range(n + 12)]
-        post = [[] for w in range(n + 12)]
-        for k in range(8):
-            g, c = k // 4, k % 4
-            w = 4 * k + 6
-            pre[w].append((f_transposes, (g, c)))
-            post[w].append((f_copy, (g, c, 0, g == 0)))
-            post[w].append((quant_tok, (g, c)))
-            post[w + 1].append((f_copy, (g, c, 1, g == 0 or k == 7)))
-            if k < 7:
-                post[w + 2].append((quant_f, (g, c)))
-            if k >= 2:
-                post[4 * (k - 2) + 1].append((load_z, (g, c, 1)))
-                post[4 * (k - 2) + 2].append((load_g, (g, c)))
-        post[2].append((load_x, (0,)))
-        post[6].append((load_vec, ()))
-        post[10].append((load_x, (1,)))
-        post[15].append((load_g0, (0,)))
-        post[23].append((load_g0, (1,)))
+        todo = [[] for w in range(n + 1)]
+
+        def at(w, fn, *args):
+            todo[w].append((fn, args))
+
+        for k in range(7):
+            g, c = ORDER[k]
+            for u in range(2):
+                at(4 * k + FT[u], f_transposes, g, c, u)
+                at(4 * k + FC[u], f_copy, g, c, u, FC_ENG[2 * k + u] == "S")
+            at(4 * k + QT, quant_tok, g, c)
+            if k < 6:
+                at(4 * k + QF, quant_f, g, c, 0, 2)
+        for g in range(NG):
+            w = H_AT[g]
+            for j in range(J):
+                at(w + j, h_sum, g, j, nc.gpsimd if H_ENG[g] == "G" else nc.vector)
+                at(w + j + 1, h_norm, g, j)
+            for i in range(2):
+                at(w + 3 + 2 * i, h_gain, g, i)
+                at(w + 6 + i, h_shift, g, i)
+            at(w + 8, h_quant, g)
         for i in range(8):
             c, k = i // 2, i % 2
-            post[3 + i].append((w_turn, (c, k)))
-            post[4 + i].append((w_copy, (c, k)))
+            w = W_AT + W_STEP * i
+            at(w, w_turn, c, k)
+            at(w + WC_LAG, w_copy, c, k, W_ENG == "S")
             if k == 1:
-                post[5 + i].append((w_quant, (c,)))
-        for g, w in ((0, 8), (1, 14)):
-            for j in range(J):
-                post[w - 1 + j].append((h_sum, (g, j)))
-                post[w + j].append((h_norm, (g, j)))
-            post[w + 2].append((h_gain, (g, 0)))
-            post[w + 4].append((h_gain, (g, 1)))
-            post[w + 5].append((h_shift, (g, 0)))
-            post[w + 5].append((h_shift, (g, 1)))
-            post[w + 6].append((h_quant, (g,)))
+                at(w + 1 + WC_LAG, w_quant, c)
         for j in range(J):
-            w = 21 + j
-            post[w].append((dg_mm, (0, j, (0, 1, 2, 3), "mm")))
-            post[w].append((dg_dn, (0, j)))
-            post[w + 1].append((dg_dot, (0, j)))
-            post[w + 2].append((dg_q, (0, j)))
-            post[w + 3].append((dg_out, (0, j)))
-        for c in range(NC):
+            w = DG_AT + DG_STEP * j
+            at(w, dg_mm, 0, j, (0, 1, 2, 3), "mm")
+            at(w + 1, dg_read, 0, j)
+            at(w + 2, dg_q, 0, j)
+            at(w + 3, dg_r, 0, j)
+            at(min(w + 3, n - 1), dg_out, 0, j, O_ENG == "V")
+        wleft = []
+        for c in range(3):
             for a in range(4):
-                w = 4 * c + 23 + a
-                if c == 3:
-                    w = 35
-                post[w].append((weight_grad, (c, a)))
+                w = WG_AT[c] + WG_STEP[c] * a
+                if w < n:
+                    at(w, weight_grad, c, a)
+                else:
+                    wleft.append((weight_grad, (c, a)))
+                if w + WO_LAG < n:
+                    at(w + WO_LAG, weight_out, c, a, WO_ENG[4 * c + a] == "S")
+                else:
+                    wleft.append((weight_out, (c, a, WO_ENG[4 * c + a] == "S")))
 
         nc.sync.dma_start(out=st[:], in_=sv)
         load_z(0, 0, 4)
-        load_g(0, 0)
         load_z(0, 1, 1)
-        load_w(0)
-        load_w(1)
+        load_g(0, 0)
         load_g(0, 1)
+        load_x(0)
+        load_vec()
+        load_x(1)
         clamp(0)
-        clamp(1)
         z_transposes(0)
-        for s in range(n + 4):
-            for f, args in pre[s]:
+        clamp(1)
+        z_transposes(1)
+        clamp(2)
+        nc.vector.tensor_scalar(
+            out=rneg[:], in0=st[:, :, :, 1], scalar1=-1.0 / D, scalar2=None, op0=ALU.mult
+        )
+        loads = {LW[0]: ((load_w, (0,)),), LW[1]: ((load_w, (1,)),), 13: ((load_g0, (0,)),), 20: ((load_g0, (1,)),)}
+        pe_fns = (f_transposes, w_turn, weight_grad, dg_mm)
+        for s in range(n):
+            if s % 4 == 1 and s // 4 + 2 < 8:
+                load_z(*ORDER[s // 4 + 2], 1)
+                load_g(*ORDER[s // 4 + 2])
+            for f, args in loads.get(s, ()):
                 f(*args)
-            if s + 1 < n:
+            if ZA == 2 and s + 2 < n:
+                z_transposes(s + 2)
+            gelus(s)
+            if ZA == 1 and 1 <= s and s + 1 < n:
                 z_transposes(s + 1)
-            if s < n:
-                gelus(s)
-                eight(s)
-            if 1 <= s <= n:
+            if PE_LATE == 0:
+                for f, args in todo[s]:
+                    if f in pe_fns:
+                        f(*args)
+            if 1 <= s:
                 negative(s - 1)
                 sums(s - 1)
-            if 2 <= s <= n + 1:
+            if PE_LATE:
+                for f, args in todo[s]:
+                    if f in pe_fns:
+                        f(*args)
+            if 2 <= s:
                 dz(s - 2)
-            if s + 2 < n:
-                clamp(s + 2)
-            for f, args in post[s]:
-                f(*args)
-            if s == n:
-                dg_mm(1, 0, (0, 1, 2), "zp")
-                dg_mm(1, 1, (0, 1, 2), "zp")
-        quant_f(1, 3)
-        dg_mm(1, 0, (3,), "zp")
-        dg_mm(1, 1, (3,), "zp")
-        dg_mm(1, 2, (0, 1, 2, 3), "dp")
-        dg_mm(1, 3, (0, 1, 2, 3), "dp")
-        dg_dn(1, 0)
-        dg_dn(1, 1)
-        dg_dot(1, 0)
-        dg_dot(1, 1)
+            if s + 3 < n:
+                clamp(s + 3)
+            for f, args in todo[s]:
+                if f not in pe_fns:
+                    f(*args)
+
+        outs = [x for x in wleft if x[0] == weight_out] + [(weight_out, (3, a, True)) for a in range(4)]
+        grads = [x for x in wleft if x[0] == weight_grad] + [(weight_grad, (3, a)) for a in range(4)]
+        lag = len(outs) - len(grads)
+
+        def products(k):
+            for i in range(k):
+                if outs and len(outs) - len(grads) >= 1:
+                    f, args = outs.pop(0)
+                    f(*args)
+                if grads:
+                    f, args = grads.pop(0)
+                    f(*args)
+
+        f_transposes(1, 3, 0)
+        negative(n - 1)
+        sums(n - 1)
+        for f, args in todo[n]:
+            f(*args)
+        if QF > 7:
+            quant_f(1, 2, 0, 2)
+        dz(n - 2)
+        f_copy(1, 3, 0, True)
+        dg_mm(1, 0, (0, 1, 2), "zp")
+        quant_f(1, 3, 0, 1)
+        dz(n - 1)
+        dg_mm(1, 0, (3,), "")
+        f_transposes(1, 3, 1)
+        products(1)
+        dg_mm(1, 1, (0, 1, 2, 3), "zp")
+        products(1)
+        f_copy(1, 3, 1, True)
+        quant_tok(1, 3)
+        dg_mm(1, 2, (0, 1, 2), "zp")
+        dg_read(1, 0)
         dg_q(1, 0)
+        dg_read(1, 1)
         dg_q(1, 1)
-        dg_dn(1, 2)
-        dg_out(1, 0)
-        dg_dot(1, 2)
-        dg_out(1, 1)
+        quant_f(1, 3, 1, 2)
+        products(1)
+        dg_r(1, 0)
+        dg_out(1, 0, False)
+        dg_mm(1, 2, (3,), "")
+        dg_mm(1, 3, (0, 1, 2, 3), "dp")
+        products(2)
+        dg_read(1, 2)
         dg_q(1, 2)
-        dg_dn(1, 3)
-        dg_dot(1, 3)
+        products(1)
+        dg_r(1, 1)
+        dg_out(1, 1, False)
+        dg_read(1, 3)
         dg_q(1, 3)
-        dg_out(1, 2)
-        dg_out(1, 3)
+        products(1)
+        dg_r(1, 2)
+        dg_out(1, 2, True)
+        products(2)
+        dg_r(1, 3)
+        dg_out(1, 3, True)
+        products(9)

@@ -23,7 +23,8 @@ NG = 2
 NC = 4
 CW = 512
 NB = 4
-REP = 2
+REP = 6
+UNIT = 16.0
 ORDER = ((0, 0), (0, 1), (1, 0), (0, 2), (0, 3), (1, 1), (1, 2), (1, 3))
 PE_LATE = 0
 ZA = 1
@@ -31,25 +32,25 @@ R_ZP = 2
 R_FT = 2
 R_MM = 2
 FT = (6, 7)
-FC = (6, 7)
-FC_ENG = "SSSSSVVVVVVSSS"
-QT = 7
+FC = (7, 8)
+FC_ENG = "SSSSSSSSSVSSVS"
+QT = 8
 QF = 8
-H_AT = (2, 8)
-H_ENG = "VV"
-W_AT = 10
+H_AT = (6, 11)
+H_ENG = "GV"
+W_AT = 12
 W_STEP = 1
 W_ENG = "S"
 DG_AT = 25
 DG_STEP = 1
-O_ENG = "V"
-WG_AT = (19, 28, 33)
-WG_STEP = (1, 1, 1)
-WO_ENG = "SVSSSSSVSSSS"
-WC_LAG = 0
-WO_LAG = 1
+O_ENG = "G"
+WG_AT = (20, 30, 34)
+WG_STEP = (1, 1, 2)
+WO_ENG = "SSVVSSVSVSVV"
+WC_LAG = 1
+KIND = "DDP" * 10 + "DD"
 LW = (8, 10)
-H1 = 2.0 ** -6.5
+H1 = 0.5 / UNIT / (REP - REP ** (1.0 / 3.0))
 H2 = H1 * REP ** (1.0 / 3.0)
 Z_MAX = 7.0
 Z_MIN = -30.0
@@ -190,25 +191,43 @@ def tile_flashinferblock_pb_v_kernel(
 
         def sums(s):
             dp[s] = psum.tile([P, J, P], F32, name="dp", tag="dp")
+            if KIND[s] == "R":
+                plus = [gel[s, 2]] * REP + [gel[s, 0]]
+            elif KIND[s] == "D":
+                t = work.tile([P, J, P], F32, name="tw", tag="tw")
+                nc.vector.tensor_scalar(
+                    out=t[:], in0=gel[s, 2][:], scalar1=float(REP), scalar2=None, op0=ALU.mult
+                )
+                plus = [t, gel[s, 0]]
+            else:
+                t = work.tile([P, J, P], F32, name="tw", tag="tw")
+                nc.vector.scalar_tensor_tensor(
+                    out=t[:].rearrange("p j f -> p (j f)"),
+                    in0=gel[s, 2][:].rearrange("p j f -> p (j f)"),
+                    scalar=float(REP),
+                    in1=gel[s, 0][:].rearrange("p j f -> p (j f)"),
+                    op0=ALU.mult,
+                    op1=ALU.add,
+                )
+                plus = [t]
             for j in range(J):
-                terms = [gel[s, 2]] * REP + [gel[s, 0], nn[s]]
+                terms = plus + [nn[s]]
                 for i, t in enumerate(terms):
                     nc.tensor.matmul(
-                        dp[s][:, j, :], lhsT=t[:, j, :], rhs=ident[:], is_transpose=True, start=(i == 0), stop=(i == REP + 1)
+                        dp[s][:, j, :], lhsT=t[:, j, :], rhs=ident[:], is_transpose=True, start=(i == 0), stop=(i == len(terms) - 1)
                     )
 
         def dz(s):
             g, c, b = gcb(s)
             if b == 0:
-                dzc[g, c] = b4.tile([P, CW, J], BF16, name="dzc", tag="b4", align_bytes=64)
+                dzc[g, c] = b4.tile([P, 4, P, J], BF16, name="dzc", tag="b4", align_bytes=64)
             js, fs = part(s)
-            nc.vector.scalar_tensor_tensor(
-                out=dzc[g, c][:, fs, js],
-                in0=dp[s][:].rearrange("p i f -> p (i f)").rearrange("p (j f) -> p f j", j=js.stop - js.start),
-                scalar=0.5 / (REP * H1 - H2),
-                in1=gt[g, c][:, js, fs].rearrange("p j f -> p f j"),
-                op0=ALU.mult,
-                op1=ALU.mult,
+            nj = js.stop - js.start
+            nc.vector.tensor_tensor(
+                out=dzc[g, c][:, :, fs.start // 4 : fs.stop // 4, js],
+                in0=dp[s][:].rearrange("p i f -> p (i f)").rearrange("p (j q t) -> p t q j", j=nj, t=4),
+                in1=gt[g, c][:, js, fs].rearrange("p j (q t) -> p t q j", t=4),
+                op=ALU.mult,
             )
 
         def quant_tok(g, c):
@@ -216,17 +235,14 @@ def tile_flashinferblock_pb_v_kernel(
                 tcodes[g, c] = work.tile([P, CW], U32, name="tc1", tag="tc1", align_bytes=64)
                 tscale[g, c] = work.tile([P, CW], U8, name="ts1", tag="ts1", align_bytes=64)
             nc.vector.quantize_mx(
-                out=tcodes[g, c][:].bitcast(E5), scales=tscale[g, c][:], in_=dzc[g, c][:].rearrange("p f j -> p (f j)")
+                out=tcodes[g, c][:].bitcast(E5), scales=tscale[g, c][:], in_=dzc[g, c][:].rearrange("p t q j -> p (t q j)")
             )
 
         def f_transposes(g, c, u):
-            words = dzc[g, c][:].rearrange("p f j -> p (f j)").bitcast(F32)
-            if (g, c, u) == (1, 3, 1):
-                tp = psum.tile([P, 4, P], F32, name="ftp2", tag="dp")
-            else:
-                tp = psum1.tile([P, 4, P], F32, name="ftp", tag="ftp")
+            words = dzc[g, c][:].rearrange("p t q j -> p (t q j)").bitcast(F32)
+            tp = psum1.tile([P, 4, P], F32, name="ftp", tag="ftp")
             for t in range(4):
-                nc.tensor.transpose(tp[:, t, :], words[:, 2 * t + u : 2 * CW : 8], ident[:])
+                nc.tensor.transpose(tp[:, t, :], words[:, 2 * P * t + u : 2 * P * (t + 1) : 2], ident[:])
             ftp[g, c, u] = tp
 
         def f_copy(g, c, u, scalar):
@@ -328,8 +344,12 @@ def tile_flashinferblock_pb_v_kernel(
         def weight_out(c, a, scalar):
             acc = wacc[c, a]
             res = work4.tile([P, CW], F32, name="res", tag="res")
-            copy = nc.scalar.copy if scalar else nc.vector.tensor_copy
-            copy(out=res[:], in_=acc[:])
+            src = acc[:].rearrange("p (t q) -> p q t", t=4)
+            dst = res[:].rearrange("p (q t) -> p q t", t=4)
+            if scalar:
+                nc.scalar.activation(out=dst, in_=src, func=ACT.Copy, scale=UNIT)
+            else:
+                nc.vector.tensor_scalar(out=dst, in0=src, scalar1=UNIT, scalar2=None, op0=ALU.mult)
             nc.sync.dma_start(out=o1v[a, :, c * CW : (c + 1) * CW], in_=res[:])
 
         dh, s12, dn, qq = {}, {}, {}, {}
@@ -424,15 +444,15 @@ def tile_flashinferblock_pb_v_kernel(
         wleft = []
         for c in range(3):
             for a in range(4):
-                w = WG_AT[c] + WG_STEP[c] * a
+                w = WG_AT[c] + WG_STEP[c] * (a // 2)
                 if w < n:
                     at(w, weight_grad, c, a)
                 else:
                     wleft.append((weight_grad, (c, a)))
-                if w + WO_LAG < n:
-                    at(w + WO_LAG, weight_out, c, a, WO_ENG[4 * c + a] == "S")
+                if w + 1 < n:
+                    at(w + 1, weight_out, c, a, WO_ENG[4 * c + a] == "S")
                 else:
-                    wleft.append((weight_out, (c, a, WO_ENG[4 * c + a] == "S")))
+                    wleft.append((weight_out, (c, a, True)))
 
         nc.sync.dma_start(out=st[:], in_=sv)
         load_z(0, 0, 4)
@@ -448,7 +468,7 @@ def tile_flashinferblock_pb_v_kernel(
         z_transposes(1)
         clamp(2)
         nc.vector.tensor_scalar(
-            out=rneg[:], in0=st[:, :, :, 1], scalar1=-1.0 / D, scalar2=None, op0=ALU.mult
+            out=rneg[:], in0=st[:, :, :, 1], scalar1=-UNIT / D, scalar2=None, op0=ALU.mult
         )
         loads = {LW[0]: ((load_w, (0,)),), LW[1]: ((load_w, (1,)),), 13: ((load_g0, (0,)),), 20: ((load_g0, (1,)),)}
         pe_fns = (f_transposes, w_turn, weight_grad, dg_mm)
@@ -495,8 +515,8 @@ def tile_flashinferblock_pb_v_kernel(
                     f, args = grads.pop(0)
                     f(*args)
 
-        f_transposes(1, 3, 0)
         negative(n - 1)
+        f_transposes(1, 3, 0)
         sums(n - 1)
         for f, args in todo[n]:
             f(*args)
@@ -505,32 +525,33 @@ def tile_flashinferblock_pb_v_kernel(
         dz(n - 2)
         f_copy(1, 3, 0, True)
         dg_mm(1, 0, (0, 1, 2), "zp")
-        quant_f(1, 3, 0, 1)
+        products(1)
         dz(n - 1)
+        quant_f(1, 3, 0, 1)
         dg_mm(1, 0, (3,), "")
         f_transposes(1, 3, 1)
-        products(1)
         dg_mm(1, 1, (0, 1, 2, 3), "zp")
-        products(1)
         f_copy(1, 3, 1, True)
-        quant_tok(1, 3)
-        dg_mm(1, 2, (0, 1, 2), "zp")
+        products(1)
         dg_read(1, 0)
         dg_q(1, 0)
+        quant_tok(1, 3)
+        dg_mm(1, 2, (0, 1, 2), "zp" if R_ZP == 3 else "dp")
         dg_read(1, 1)
         dg_q(1, 1)
         quant_f(1, 3, 1, 2)
+        dg_mm(1, 2, (3,), "")
+        dg_mm(1, 3, (0, 1, 2, 3), "dp")
         products(1)
         dg_r(1, 0)
         dg_out(1, 0, False)
-        dg_mm(1, 2, (3,), "")
-        dg_mm(1, 3, (0, 1, 2, 3), "dp")
-        products(2)
+        products(1)
         dg_read(1, 2)
         dg_q(1, 2)
         products(1)
         dg_r(1, 1)
         dg_out(1, 1, False)
+        products(1)
         dg_read(1, 3)
         dg_q(1, 3)
         products(1)

from contextlib import ExitStack

import concourse.mybir as mybir
from concourse.masks import make_identity

B, S, D, F = 4, 256, 512, 2048
T = B * S
FLOPS = 2 * 2 * T * D * F
BYTES = 25176064

F32 = mybir.dt.float32
BF16 = mybir.dt.bfloat16
U32 = mybir.dt.uint32
U8 = mybir.dt.uint8
E4 = mybir.dt.float8_e4m3fn_x4
E5 = mybir.dt.float8_e5m2_x4
ALU = mybir.AluOpType
ACT = mybir.ActivationFunctionType

P = 128
J = 4
NG = 2
NC = 4
CW = 512
NB = 4
REP = 6
UNIT = 16.0
ORDER = ((0, 0), (0, 1), (1, 0), (0, 2), (0, 3), (1, 1), (1, 2), (1, 3))
PE_LATE = 0
ZA = 1
R_ZP = 2
R_FT = 2
R_MM = 2
FT = (6, 7)
FC = (7, 8)
FC_ENG = "SSSSSSSSSVSSVS"
QT = 8
QF = 8
H_AT = (6, 11)
H_ENG = "GV"
W_AT = 12
W_STEP = 1
W_ENG = "S"
DG_AT = 25
DG_STEP = 1
O_ENG = "G"
WG_AT = (20, 30, 34)
WG_STEP = (1, 1, 2)
WO_ENG = "SSVVSSVSVSVV"
WC_LAG = 1
KIND = "DDP" * 10 + "DD"
LW = (8, 10)
H1 = 0.5 / UNIT / (REP - REP ** (1.0 / 3.0))
H2 = H1 * REP ** (1.0 / 3.0)
Z_MAX = 7.0
Z_MIN = -30.0


def tile_flashinferblock_pb_v_kernel(
    tc, attn_out, x, w_proj, b_proj, g2, beta2, w_fc1, b_fc1, proj, stats, z, grad_0, grad_1, out_0, out_1
):
    nc = tc.nc

    def tok(ap):
        return ap.flatten_outer_dims().rearrange("(g p j) f -> g p j f", g=NG, j=J)

    zv, gv, xv, pv, g0v, ov = tok(z), tok(grad_1), tok(x), tok(proj), tok(grad_0), tok(out_0)
    sv = stats.flatten_outer_dims().rearrange("(g p j) s -> p g j s", g=NG, j=J)
    wv = w_fc1.rearrange("(a p) f -> p a f", p=P)
    o1v = out_1.rearrange("(a p) f -> a p f", p=P)

    with ExitStack() as ctx:
        keep = ctx.enter_context(tc.tile_pool(name="keep", bufs=1))
        st8 = ctx.enter_context(tc.tile_pool(name="st8", bufs=6))
        st4 = ctx.enter_context(tc.tile_pool(name="st4", bufs=6))
        b4 = ctx.enter_context(tc.tile_pool(name="b4", bufs=6))
        work = ctx.enter_context(tc.tile_pool(name="work", bufs=2))
        work3 = ctx.enter_context(tc.tile_pool(name="work3", bufs=3))
        work4 = ctx.enter_context(tc.tile_pool(name="work4", bufs=4))
        psum = ctx.enter_context(tc.psum_pool(name="psum", bufs=2))
        psum3 = ctx.enter_context(tc.psum_pool(name="psum3", bufs=R_ZP))
        psum1 = ctx.enter_context(tc.psum_pool(name="psum1", bufs=R_FT))
        psumm = ctx.enter_context(tc.psum_pool(name="psumm", bufs=R_MM))

        ident = keep.tile([P, P], F32, name="ident")
        make_identity(nc, ident[:])
        warm = keep.tile([P, 1], F32, name="warm")
        nc.vector.memset(warm[:], 0.0)
        nc.scalar.activation(out=warm[:], in_=warm[:], func=ACT.Gelu)

        st = keep.tile([P, NG, J, 2], F32, name="st")
        g2b = keep.tile([P, D], BF16, name="g2b")
        b2b = keep.tile([P, D], BF16, name="b2b")
        xhat = keep.tile([P, NG, J, D], F32, name="xhat")
        hg = keep.tile([P, NG, J, D], F32, name="hg")
        rneg = keep.tile([P, NG, J], F32, name="rneg")
        hcodes = keep.tile([P, NG, D], U32, name="hcodes", align_bytes=64)
        hscale = keep.tile([P, NG, D], U8, name="hscale", align_bytes=64)
        wcodes = keep.tile([P, NC, D], U32, name="wcodes", align_bytes=64)
        wscale = keep.tile([P, NC, D], U8, name="wscale", align_bytes=64)
        fcodes, fscale, tcodes, tscale = {}, {}, {}, {}
        zt, gt, xt, pt, g0t, wt = {}, {}, {}, {}, {}, {}
        for g in range(NG):
            for c in range(NC):
                fcodes[g, c] = keep.tile([P, CW], U32, name="fc%d%d" % (g, c), align_bytes=64)
                fscale[g, c] = keep.tile([P, CW], U8, name="fs%d%d" % (g, c), align_bytes=64)
        for c in range(NC):
            tcodes[0, c] = keep.tile([P, CW], U32, name="tc%d" % c, align_bytes=64)
            tscale[0, c] = keep.tile([P, CW], U8, name="ts%d" % c, align_bytes=64)

        ctx.enter_context(tc.manual_schedule())

        def load_z(g, c, pieces):
            a = st8.tile([P, J, CW], F32, name="zc", tag="s8")
            w = CW // pieces
            for i in range(pieces):
                nc.sync.dma_start(
                    out=a[:, :, i * w : (i + 1) * w], in_=zv[g, :, :, c * CW + i * w : c * CW + (i + 1) * w]
                )
            zt[g, c] = a

        def load_g(g, c):
            b = st4.tile([P, J, CW], BF16, name="gc", tag="s4")
            nc.sync.dma_start(out=b[:], in_=gv[g, :, :, c * CW : (c + 1) * CW])
            gt[g, c] = b

        def load_w(k):
            a = st8.tile([P, 2, F], BF16, name="wr", tag="s8")
            nc.sync.dma_start(out=a[:], in_=wv[:, 2 * k : 2 * k + 2, :])
            wt[k] = a

        def load_x(g):
            a = st4.tile([P, J, D], BF16, name="xr", tag="s4")
            nc.sync.dma_start(out=a[:], in_=xv[g])
            b = st8.tile([P, J, D], F32, name="pr", tag="s8")
            nc.sync.dma_start(out=b[:], in_=pv[g])
            xt[g] = a
            pt[g] = b

        def load_g0(g):
            a = st4.tile([P, J, D], BF16, name="g0", tag="s4")
            nc.sync.dma_start(out=a[:], in_=g0v[g])
            g0t[g] = a

        def load_vec():
            nc.sync.dma_start(out=g2b[:], in_=g2.partition_broadcast(P))
            nc.sync.dma_start(out=b2b[:], in_=beta2.partition_broadcast(P))

        gel, nn, zp, dp, dzc, ftp, dzf = {}, {}, {}, {}, {}, {}, {}

        def gcb(s):
            return ORDER[s // 4] + (s % 4,)

        def part(s):
            b = s % 4
            if s // 4 < 7:
                return slice(0, 4), slice(b * P, (b + 1) * P)
            return slice(b // 2 * 2, b // 2 * 2 + 2), slice(b % 2 * 2 * P, (b % 2 * 2 + 2) * P)

        def clamp(s):
            g, c, b = gcb(s)
            js, fs = part(s)
            a = zt[g, c][:, js, fs]
            nc.vector.tensor_scalar(out=a, in0=a, scalar1=Z_MAX, scalar2=Z_MIN, op0=ALU.min, op1=ALU.max)

        def z_transposes(s):
            g, c, b = gcb(s)
            zp[s] = psum3.tile([P, J, P], F32, name="zp", tag="zp")
            js, fs = part(s)
            blocks = [(j, f) for j in range(js.start, js.stop) for f in range(fs.start, fs.stop, P)]
            for i, (j, f) in enumerate(blocks):
                nc.tensor.transpose(zp[s][:, i, :], zt[g, c][:, j, f : f + P], ident[:])

        def gelus(s):
            src = zp[s][:].rearrange("p j f -> p (j f)")
            for k, off in ((1, -H1), (3, H2), (2, H1), (0, -H2)):
                t = work3.tile([P, J, P], F32, name="ge%d" % k, tag="ge%d" % k)
                nc.scalar.activation(out=t[:].rearrange("p j f -> p (j f)"), in_=src, func=ACT.Gelu, bias=off)
                gel[s, k] = t

        def negative(s):
            nn[s] = work.tile([P, J, P], F32, name="nn", tag="nn")
            nc.vector.scalar_tensor_tensor(
                out=nn[s][:].rearrange("p j f -> p (j f)"),
                in0=gel[s, 1][:].rearrange("p j f -> p (j f)"),
                scalar=-float(REP),
                in1=gel[s, 3][:].rearrange("p j f -> p (j f)"),
                op0=ALU.mult,
                op1=ALU.subtract,
            )

        def sums(s):
            dp[s] = psum.tile([P, J, P], F32, name="dp", tag="dp")
            if KIND[s] == "R":
                plus = [gel[s, 2]] * REP + [gel[s, 0]]
            elif KIND[s] == "D":
                t = work.tile([P, J, P], F32, name="tw", tag="tw")
                nc.vector.tensor_scalar(
                    out=t[:], in0=gel[s, 2][:], scalar1=float(REP), scalar2=None, op0=ALU.mult
                )
                plus = [t, gel[s, 0]]
            else:
                t = work.tile([P, J, P], F32, name="tw", tag="tw")
                nc.vector.scalar_tensor_tensor(
                    out=t[:].rearrange("p j f -> p (j f)"),
                    in0=gel[s, 2][:].rearrange("p j f -> p (j f)"),
                    scalar=float(REP),
                    in1=gel[s, 0][:].rearrange("p j f -> p (j f)"),
                    op0=ALU.mult,
                    op1=ALU.add,
                )
                plus = [t]
            for j in range(J):
                terms = plus + [nn[s]]
                for i, t in enumerate(terms):
                    nc.tensor.matmul(
                        dp[s][:, j, :], lhsT=t[:, j, :], rhs=ident[:], is_transpose=True, start=(i == 0), stop=(i == len(terms) - 1)
                    )

        def dz(s):
            g, c, b = gcb(s)
            if b == 0:
                dzc[g, c] = b4.tile([P, 4, P, J], BF16, name="dzc", tag="b4", align_bytes=64)
            js, fs = part(s)
            nj = js.stop - js.start
            nc.vector.tensor_tensor(
                out=dzc[g, c][:, :, fs.start // 4 : fs.stop // 4, js],
                in0=dp[s][:].rearrange("p i f -> p (i f)").rearrange("p (j q t) -> p t q j", j=nj, t=4),
                in1=gt[g, c][:, js, fs].rearrange("p j (q t) -> p t q j", t=4),
                op=ALU.mult,
            )

        def quant_tok(g, c):
            if g == 1:
                tcodes[g, c] = work.tile([P, CW], U32, name="tc1", tag="tc1", align_bytes=64)
                tscale[g, c] = work.tile([P, CW], U8, name="ts1", tag="ts1", align_bytes=64)
            nc.vector.quantize_mx(
                out=tcodes[g, c][:].bitcast(E5), scales=tscale[g, c][:], in_=dzc[g, c][:].rearrange("p t q j -> p (t q j)")
            )

        def f_transposes(g, c, u):
            words = dzc[g, c][:].rearrange("p t q j -> p (t q j)").bitcast(F32)
            tp = psum1.tile([P, 4, P], F32, name="ftp", tag="ftp")
            for t in range(4):
                nc.tensor.transpose(tp[:, t, :], words[:, 2 * P * t + u : 2 * P * (t + 1) : 2], ident[:])
            ftp[g, c, u] = tp

        def f_copy(g, c, u, scalar):
            if (g, c) not in dzf:
                dzf[g, c] = b4.tile([P, 2, 2, P, 4], BF16, name="dzf", tag="b4", align_bytes=64)
            src = ftp[g, c, u][:].rearrange("p t r -> p (t r)").bitcast(BF16)
            src = src.rearrange("p (t r e) -> p e r t", t=4, e=2)
            if scalar:
                nc.scalar.copy(out=dzf[g, c][:, u], in_=src)
            else:
                nc.vector.tensor_copy(out=dzf[g, c][:, u], in_=src)

        def quant_f(g, c, lo, hi):
            nc.vector.quantize_mx(
                out=fcodes[g, c][:, 2 * P * lo : 2 * P * hi].bitcast(E5),
                scales=fscale[g, c][:, 2 * P * lo : 2 * P * hi],
                in_=dzf[g, c][:, lo:hi].rearrange("p u e r t -> p (u e r t)"),
            )

        wg = {}
        wtp = {}

        def w_turn(c, k):
            if k == 0:
                wg[c] = b4.tile([P, 4, P, 4], BF16, name="wg", tag="b4", align_bytes=64)
            tp = psum1.tile([P, 2, 2, P], F32, name="wtp", tag="ftp")
            for a in range(2):
                words = wt[k][:, a, :].bitcast(F32)
                for u in range(2):
                    nc.tensor.transpose(tp[:, a, u, :], words[:, 256 * c + u : 256 * (c + 1) : 2], ident[:])
            wtp[c, k] = tp

        def w_copy(c, k, scalar):
            dst = wg[c][:].rearrange("p a r t -> p (a r t)").bitcast(F32)
            dst = dst.rearrange("p (a r u) -> p a r u", a=4, u=2)
            copy = nc.scalar.copy if scalar else nc.vector.tensor_copy
            copy(out=dst[:, 2 * k : 2 * k + 2], in_=wtp[c, k][:].rearrange("p a u r -> p a r u"))

        def w_quant(c):
            nc.vector.quantize_mx(
                out=wcodes[:, c, :].bitcast(E4), scales=wscale[:, c, :], in_=wg[c][:].rearrange("p a r t -> p (a r t)")
            )

        hb = {}

        def h_sum(g, j, eng):
            eng.tensor_tensor(out=pt[g][:, j, :], in0=pt[g][:, j, :], in1=xt[g][:, j, :], op=ALU.add)

        def h_norm(g, j):
            nc.vector.tensor_scalar(
                out=xhat[:, g, j, :],
                in0=pt[g][:, j, :],
                scalar1=st[:, g, j, 0:1],
                scalar2=st[:, g, j, 1:2],
                op0=ALU.subtract,
                op1=ALU.mult,
            )

        def h_gain(g, k):
            nc.vector.tensor_tensor(
                out=hg[:, g, 2 * k : 2 * k + 2],
                in0=xhat[:, g, 2 * k : 2 * k + 2],
                in1=g2b[:].unsqueeze(1).to_broadcast([P, 2, D]),
                op=ALU.mult,
            )

        def h_shift(g, k):
            if k == 0:
                hb[g] = b4.tile([P, D, J], BF16, name="hb", tag="b4", align_bytes=64)
            w = slice(k * (D // 2), (k + 1) * (D // 2))
            nc.vector.tensor_tensor(
                out=hb[g][:, w],
                in0=hg[:, g, :, w].rearrange("p j d -> p d j"),
                in1=b2b[:, w].unsqueeze(2).to_broadcast([P, D // 2, J]),
                op=ALU.add,
            )

        def h_quant(g):
            nc.vector.quantize_mx(
                out=hcodes[:, g, :].bitcast(E4), scales=hscale[:, g, :], in_=hb[g][:].rearrange("p d j -> p (d j)")
            )

        wacc = {}

        def weight_grad(c, a):
            acc = psumm.tile([P, CW], F32, name="acc", tag="mm")
            for g in range(NG):
                nc.tensor.matmul_mx(
                    out=acc[:],
                    lhsT=hcodes[:, g, a * P : (a + 1) * P].bitcast(E4),
                    lhsT_scale=hscale[:, g, a * P : (a + 1) * P],
                    rhs=tcodes[g, c][:].bitcast(E5),
                    rhs_scale=tscale[g, c][:],
                    start=(g == 0),
                    stop=(g == NG - 1),
                )
            wacc[c, a] = acc

        def weight_out(c, a, scalar):
            acc = wacc[c, a]
            res = work4.tile([P, CW], F32, name="res", tag="res")
            src = acc[:].rearrange("p (t q) -> p q t", t=4)
            dst = res[:].rearrange("p (q t) -> p q t", t=4)
            if scalar:
                nc.scalar.activation(out=dst, in_=src, func=ACT.Copy, scale=UNIT)
            else:
                nc.vector.tensor_scalar(out=dst, in0=src, scalar1=UNIT, scalar2=None, op0=ALU.mult)
            nc.sync.dma_start(out=o1v[a, :, c * CW : (c + 1) * CW], in_=res[:])

        dh, s12, dn, qq = {}, {}, {}, {}

        def dg_mm(g, j, cs, tag):
            if cs[0] == 0:
                dh[g, j] = {"zp": psum3, "dp": psum, "mm": psumm}[tag].tile([P, D], F32, name="dh", tag=tag)
            for c in cs:
                nc.tensor.matmul_mx(
                    out=dh[g, j][:],
                    lhsT=fcodes[g, c][:, j * P : (j + 1) * P].bitcast(E5),
                    lhsT_scale=fscale[g, c][:, j * P : (j + 1) * P],
                    rhs=wcodes[:, c, :].bitcast(E4),
                    rhs_scale=wscale[:, c, :],
                    start=(c == 0),
                    stop=(c == NC - 1),
                )

        def dg_read(g, j):
            s12[g, j] = work3.tile([P, 8], F32, name="s12", tag="s12")
            dn[g, j] = work3.tile([P, D], F32, name="dn", tag="dn")
            junk = work.tile([P, D], F32, name="junk", tag="nn")
            for i, (dst, row) in enumerate(((dn[g, j], g2b[:]), (junk, hg[:, g, j, :]))):
                nc.vector.scalar_tensor_tensor(
                    out=dst[:],
                    in0=dh[g, j][:],
                    scalar=rneg[:, g, j : j + 1],
                    in1=row,
                    op0=ALU.mult,
                    op1=ALU.mult,
                    accum_out=s12[g, j][:, i : i + 1],
                )

        def dg_q(g, j):
            qq[g, j] = work4.tile([P, D], F32, name="q", tag="q")
            nc.scalar.activation(
                out=qq[g, j][:],
                in_=xhat[:, g, j, :],
                func=ACT.Identity,
                scale=s12[g, j][:, 1:2],
                bias=s12[g, j][:, 0:1],
            )

        def dg_r(g, j):
            nc.vector.scalar_tensor_tensor(
                out=qq[g, j][:], in0=dn[g, j][:], scalar=-float(D), in1=qq[g, j][:], op0=ALU.mult, op1=ALU.add
            )

        def dg_out(g, j, vector):
            eng = nc.vector if vector else nc.gpsimd
            o = work4.tile([P, D], F32, name="o", tag="q")
            eng.tensor_tensor(out=o[:], in0=qq[g, j][:], in1=g0t[g][:, j, :], op=ALU.add)
            nc.sync.dma_start(out=ov[g, :, j, :], in_=o[:])

        n = NG * NC * NB
        todo = [[] for w in range(n + 1)]

        def at(w, fn, *args):
            todo[w].append((fn, args))

        for k in range(7):
            g, c = ORDER[k]
            for u in range(2):
                at(4 * k + FT[u], f_transposes, g, c, u)
                at(4 * k + FC[u], f_copy, g, c, u, FC_ENG[2 * k + u] == "S")
            at(4 * k + QT, quant_tok, g, c)
            if k < 6:
                at(4 * k + QF, quant_f, g, c, 0, 2)
        for g in range(NG):
            w = H_AT[g]
            for j in range(J):
                at(w + j, h_sum, g, j, nc.gpsimd if H_ENG[g] == "G" else nc.vector)
                at(w + j + 1, h_norm, g, j)
            for i in range(2):
                at(w + 3 + 2 * i, h_gain, g, i)
                at(w + 6 + i, h_shift, g, i)
            at(w + 8, h_quant, g)
        for i in range(8):
            c, k = i // 2, i % 2
            w = W_AT + W_STEP * i
            at(w, w_turn, c, k)
            at(w + WC_LAG, w_copy, c, k, W_ENG == "S")
            if k == 1:
                at(w + 1 + WC_LAG, w_quant, c)
        for j in range(J):
            w = DG_AT + DG_STEP * j
            at(w, dg_mm, 0, j, (0, 1, 2, 3), "mm")
            at(w + 1, dg_read, 0, j)
            at(w + 2, dg_q, 0, j)
            at(w + 3, dg_r, 0, j)
            at(min(w + 3, n - 1), dg_out, 0, j, O_ENG == "V")
        wleft = []
        for c in range(3):
            for a in range(4):
                w = WG_AT[c] + WG_STEP[c] * (a // 2)
                if w < n:
                    at(w, weight_grad, c, a)
                else:
                    wleft.append((weight_grad, (c, a)))
                if w + 1 < n:
                    at(w + 1, weight_out, c, a, WO_ENG[4 * c + a] == "S")
                else:
                    wleft.append((weight_out, (c, a, True)))

        nc.sync.dma_start(out=st[:], in_=sv)
        load_z(0, 0, 4)
        load_z(0, 1, 1)
        load_g(0, 0)
        load_g(0, 1)
        load_x(0)
        load_vec()
        load_x(1)
        clamp(0)
        z_transposes(0)
        clamp(1)
        z_transposes(1)
        clamp(2)
        nc.vector.tensor_scalar(
            out=rneg[:], in0=st[:, :, :, 1], scalar1=-UNIT / D, scalar2=None, op0=ALU.mult
        )
        loads = {LW[0]: ((load_w, (0,)),), LW[1]: ((load_w, (1,)),), 13: ((load_g0, (0,)),), 20: ((load_g0, (1,)),)}
        pe_fns = (f_transposes, w_turn, weight_grad, dg_mm)
        for s in range(n):
            if s % 4 == 1 and s // 4 + 2 < 8:
                load_z(*ORDER[s // 4 + 2], 1)
                load_g(*ORDER[s // 4 + 2])
            for f, args in loads.get(s, ()):
                f(*args)
            if ZA == 2 and s + 2 < n:
                z_transposes(s + 2)
            gelus(s)
            if ZA == 1 and 1 <= s and s + 1 < n:
                z_transposes(s + 1)
            if PE_LATE == 0:
                for f, args in todo[s]:
                    if f in pe_fns:
                        f(*args)
            if 1 <= s:
                negative(s - 1)
                sums(s - 1)
            if PE_LATE:
                for f, args in todo[s]:
                    if f in pe_fns:
                        f(*args)
            if 2 <= s:
                dz(s - 2)
            if s + 3 < n:
                clamp(s + 3)
            for f, args in todo[s]:
                if f not in pe_fns:
                    f(*args)

        outs = [x for x in wleft if x[0] == weight_out] + [(weight_out, (3, a, True)) for a in range(4)]
        grads = [x for x in wleft if x[0] == weight_grad] + [(weight_grad, (3, a)) for a in range(4)]
        lag = len(outs) - len(grads)

        def products(k):
            for i in range(k):
                if outs and len(outs) - len(grads) >= 1:
                    f, args = outs.pop(0)
                    f(*args)
                if grads:
                    f, args = grads.pop(0)
                    f(*args)

        negative(n - 1)
        f_transposes(1, 3, 0)
        sums(n - 1)
        for f, args in todo[n]:
            f(*args)
        if QF > 7:
            quant_f(1, 2, 0, 2)
        dz(n - 2)
        f_copy(1, 3, 0, True)
        dg_mm(1, 0, (0, 1, 2), "zp")
        products(1)
        dz(n - 1)
        quant_f(1, 3, 0, 1)
        dg_mm(1, 0, (3,), "")
        f_transposes(1, 3, 1)
        dg_mm(1, 1, (0, 1, 2, 3), "zp")
        f_copy(1, 3, 1, True)
        products(1)
        dg_read(1, 0)
        dg_q(1, 0)
        quant_tok(1, 3)
        dg_mm(1, 2, (0, 1, 2), "zp" if R_ZP == 3 else "dp")
        dg_read(1, 1)
        dg_q(1, 1)
        quant_f(1, 3, 1, 2)
        dg_mm(1, 2, (3,), "")
        dg_mm(1, 3, (0, 1, 2, 3), "dp")
        products(1)
        dg_r(1, 0)
        dg_out(1, 0, False)
        products(1)
        dg_read(1, 2)
        dg_q(1, 2)
        products(1)
        dg_r(1, 1)
        dg_out(1, 1, False)
        products(1)
        dg_read(1, 3)
        dg_q(1, 3)
        products(1)
        dg_r(1, 2)
        dg_out(1, 2, True)
        products(2)
        dg_r(1, 3)
        dg_out(1, 3, True)
        products(9)
